import numpy as np
import ml_dtypes


def mxq(x, axis, fmt="e4m3"):
    dtype, down = {"e4m3": (ml_dtypes.float8_e4m3fn, 7), "e5m2": (ml_dtypes.float8_e5m2, 14)}[fmt]
    v = np.moveaxis(np.asarray(x, np.float32).astype(ml_dtypes.bfloat16).astype(np.float64), axis, -1)
    blocks = v.reshape(v.shape[:-1] + (-1, 32))
    amax = np.abs(blocks).max(-1, keepdims=True)
    byte = np.maximum(np.where(amax > 0, np.frexp(amax)[1] - 1 + 127, 0) - down, 1)
    scale = np.exp2(byte - 127.0)
    codes = (blocks / scale).astype(np.float32).astype(dtype).astype(np.float64)
    return np.moveaxis((codes * scale).reshape(v.shape), -1, axis)


WIDE = False


def mx_kscale(k):
    if not WIDE:
        return np.ones(k)
    levels = np.array([10, -10, 5, -5, 0])
    a = np.random.permutation(np.resize(levels, k // 512 * 4)).reshape(k // 512, 4)
    idx = np.arange(k)
    return np.exp2(a[idx // 512, idx % 128 // 32])


BF16 = ml_dtypes.bfloat16


def bf(x):
    return np.asarray(x, np.float32).astype(BF16)


def f64(x):
    return np.asarray(x).astype(np.float64)


E2M1 = np.array([0.0, 0.5, 1.0, 1.5, 2.0, 3.0, 4.0, 6.0, -0.0, -0.5, -1.0, -1.5, -2.0, -3.0, -4.0, -6.0])


def pack_weight(w, fmt):
    k, n = w.shape
    w = f64(bf(w)).reshape(k // 32, 32, n)
    amax = np.abs(w).max(1)
    if fmt == "e4m3":
        byte = np.frexp(amax)[1] - 1 + 127 - 7
    else:
        mant, ex = np.frexp(amax / 6.0)
        byte = np.where(mant > 0.5, ex, ex - 1) + 127
    byte = np.clip(np.where(amax > 0, byte, 1), 1, 254)
    scaled = (w * np.exp2(127.0 - byte)[:, None, :]).reshape(k, n).astype(np.float32)
    by_word = np.ascontiguousarray(scaled.reshape(k // 512, 128, 4, n).transpose(0, 1, 3, 2))
    if fmt == "e4m3":
        words = by_word.astype(ml_dtypes.float8_e4m3fn).view(np.uint8)
    else:
        c = by_word.astype(ml_dtypes.float4_e2m1fn).view(np.uint8) & 0xF
        words = c[..., 0::2] | (c[..., 1::2] << 4)
    return np.ascontiguousarray(words), np.ascontiguousarray(byte.astype(np.uint8).reshape(k // 512, 16, n))


def unpack_weight(words, scales, fmt):
    g, p, n, _ = words.shape
    if fmt == "e4m3":
        vals = np.ascontiguousarray(words).view(ml_dtypes.float8_e4m3fn).astype(np.float64)
    else:
        nib = np.empty((g, p, n, 4), np.uint8)
        nib[..., 0::2] = words & 0xF
        nib[..., 1::2] = words >> 4
        vals = E2M1[nib]
    vals = vals * np.repeat(np.exp2(scales.astype(np.float64) - 127.0), 8, axis=1)[..., None]
    return vals.transpose(0, 1, 3, 2).reshape(g * 512, n)

def pack4(w):
    words, scales = pack_weight(w, "e2m1")
    return words.reshape(words.shape[0], 128, -1), scales


def unpack4(words, scales):
    return unpack_weight(words.reshape(words.shape[0], 128, -1, 2), scales, "e2m1")


B, C, E, H, HS, WS = 2, 512, 1536, 16, 32, 32
N = HS * WS
EPS = 1e-5
A = 2.0 * (E / H) ** -0.5 / np.sqrt(N)


def chan_layernorm(x, g):
    mean = x.mean(axis=1, keepdims=True)
    var = x.var(axis=1, keepdims=True)
    return (x - mean) * (1.0 / np.sqrt(var + EPS)) * g


def setup_inputs():
    s = mx_kscale(E)
    h_attn = bf(np.random.standard_normal((B, E, HS, WS)) * A * s[None, :, None, None])
    xn = bf(np.random.standard_normal((B, C, HS, WS)))
    wout = np.random.standard_normal((C, E)) / (np.sqrt(E) * A) / s[None, :]
    words, scales = pack4(np.ascontiguousarray(wout.T))
    bout = bf(0.3 * np.random.standard_normal(C))
    outnorm_g = bf(1.0 + 0.1 * np.random.standard_normal((1, C, 1, 1)))
    return {"h_attn": h_attn,
            "xn": xn,
            "Wout_words": words,
            "Wout_scales": scales,
            "bout": bout,
            "outnorm_g": outnorm_g}


def reference(h_attn, xn, Wout_words, Wout_scales, bout, outnorm_g):
    a = f64(h_attn).reshape(B, E, N)
    y = (unpack4(Wout_words, Wout_scales).T @ mxq(a, 1, "e4m3")) + f64(bout)[None, :, None]
    y = y.reshape(B, C, HS, WS)
    return chan_layernorm(y, f64(outnorm_g)) + f64(xn)

@@ -1,0 +1,252 @@
+from contextlib import ExitStack
+
+import concourse.mybir as mybir
+from concourse.masks import make_identity
+
+F32 = mybir.dt.float32
+BF16 = mybir.dt.bfloat16
+I32 = mybir.dt.int32
+U32 = mybir.dt.uint32
+U8 = mybir.dt.uint8
+FP8X4 = mybir.dt.float8_e4m3fn_x4
+FP4X4 = mybir.dt.float4_e2m1fn_x4
+ALU = mybir.AluOpType
+ACT = mybir.ActivationFunctionType
+
+P = 128
+PACK = 4
+K_PASS = P * PACK
+
+IMAGES = 2
+K = 1536
+PASSES = K // K_PASS
+CHANNELS = 512
+CHANNEL_TILES = CHANNELS // P
+POSITIONS = 1024
+CHUNK = 512
+POSITION_TILES = CHUNK // P
+CHUNKS_PER_IMAGE = POSITIONS // CHUNK
+CHUNKS = IMAGES * CHUNKS_PER_IMAGE
+VECTOR_SHARE = CHUNK // 2
+RUN = 4
+EPS = 1e-5
+
+FLOPS = 2 * IMAGES * POSITIONS * CHANNELS * K
+
+
+def tile_linearattention_pb_kernel(tc, h_attn, xn, Wout_words, Wout_scales, bout, outnorm_g, out):
+    nc = tc.nc
+    h_dram = h_attn.rearrange("b k h w -> b k (h w)")
+    xn_dram = xn.rearrange("b c h w -> b c (h w)")
+    out_dram = out.rearrange("b c h w -> b c (h w)")
+
+    with ExitStack() as ctx:
+        consts = ctx.enter_context(tc.tile_pool(name="consts", bufs=1))
+        raw_pool = ctx.enter_context(tc.tile_pool(name="raw", bufs=CHUNKS))
+        xn_pool = ctx.enter_context(tc.tile_pool(name="xn", bufs=IMAGES))
+        work = ctx.enter_context(tc.tile_pool(name="work", bufs=2))
+        scratch = ctx.enter_context(tc.tile_pool(name="scratch", bufs=POSITION_TILES))
+        psum_y = ctx.enter_context(tc.psum_pool(name="psum_y", bufs=POSITION_TILES))
+        psum_t = ctx.enter_context(tc.psum_pool(name="psum_t", bufs=CHANNEL_TILES))
+        ctx.enter_context(tc.manual_schedule())
+
+        ident_f32 = consts.tile([P, P], F32)
+        make_identity(nc, ident_f32[:])
+        ident_bf16 = consts.tile([P, P], BF16)
+        make_identity(nc, ident_bf16[:])
+        ones = consts.tile([P, P], BF16)
+        nc.vector.memset(ones[:], 1.0)
+        eps = consts.tile([P, 1], F32)
+        nc.vector.memset(eps[:], EPS)
+        warm = consts.tile([P, 1], F32)
+        nc.scalar.activation(out=warm[:], in_=eps[:], func=ACT.Sqrt)
+
+        rows = consts.tile([P, CHANNELS + P], BF16)
+        nc.vector.memset(rows[:], 0.0)
+        nc.sync.dma_start(out=rows[0:1, 0:CHANNELS], in_=bout.rearrange("(o c) -> o c", o=1))
+        nc.sync.dma_start(
+            out=rows[0:CHANNEL_TILES, CHANNELS:],
+            in_=outnorm_g.rearrange("o (t p) h w -> (o t) (p h w)", p=P),
+        )
+
+        raw = []
+        xn_sb = []
+
+        def image_and_columns(c):
+            first = (c % CHUNKS_PER_IMAGE) * CHUNK
+            return c // CHUNKS_PER_IMAGE, slice(first, first + CHUNK)
+
+        def load_chunk(c):
+            b, cols = image_and_columns(c)
+            raw_c = raw_pool.tile([P, PASSES, PACK, CHUNK], BF16, name="raw_c")
+            for g in range(PASSES):
+                k_rows = slice(g * K_PASS, (g + 1) * K_PASS)
+                nc.sync.dma_start(
+                    out=raw_c[:, g, :, :],
+                    in_=h_dram[b, k_rows, cols].rearrange("(p t) w -> p t w", t=PACK),
+                )
+            raw.append(raw_c)
+
+        def load_residual(b):
+            xn_b = xn_pool.tile([P, CHANNEL_TILES, POSITIONS], BF16, name="xn_b")
+            nc.sync.dma_start(out=xn_b[:], in_=xn_dram[b].rearrange("(ct p) w -> p ct w", p=P))
+            xn_sb.append(xn_b)
+
+        load_chunk(0)
+
+        w_words = consts.tile([P, PASSES, 2 * CHANNELS], U8, align_bytes=64)
+        nc.sync.dma_start(
+            out=w_words[:].bitcast(I32), in_=Wout_words.bitcast(I32).rearrange("g p n -> p g n")
+        )
+        w_scales = consts.tile([P, PASSES, CHANNELS], U8, align_bytes=64)
+        nc.vector.memset(w_scales[:].bitcast(I32), 0)
+        for quadrant in range(4):
+            nc.sync.dma_start(
+                out=w_scales[32 * quadrant : 32 * quadrant + 4, :, :].bitcast(I32),
+                in_=Wout_scales[:, 4 * quadrant : 4 * quadrant + 4, :]
+                .bitcast(I32)
+                .rearrange("g r n -> r g n"),
+            )
+
+        load_chunk(1)
+        load_residual(0)
+        load_chunk(2)
+        load_chunk(3)
+        load_residual(1)
+
+        bias_ps = psum_y.tile([P, CHANNELS], F32, name="y_ps")
+        nc.tensor.matmul(bias_ps[:], lhsT=ones[:], rhs=rows[:, 0:CHANNELS], start=True, stop=True)
+        bias = consts.tile([P, CHANNELS], F32)
+        nc.vector.tensor_copy(out=bias[:], in_=bias_ps[:])
+        gain_ps = psum_t.tile([P, P], BF16, name="zT_ps")
+        nc.tensor.transpose(gain_ps[:], rows[:, CHANNELS:], ident_bf16[:])
+        gain = consts.tile([P, CHANNEL_TILES], F32)
+        nc.vector.tensor_copy(out=gain[:], in_=gain_ps[:, 0:CHANNEL_TILES])
+
+        codes, planes, y_ps, y_sb, z_sb, zT_ps = {}, {}, {}, {}, {}, {}
+        neg_mean, rstd, shift = {}, {}, {}
+
+        def quantise(c):
+            grouped = work.tile([P, PASSES, CHUNK, PACK], BF16, name="grouped", align_bytes=64)
+            codes[c] = work.tile([P, PASSES, CHUNK], U32, name="codes", align_bytes=64)
+            planes[c] = work.tile([P, PASSES, CHUNK], U8, name="planes", align_bytes=64)
+
+            def regroup(g):
+                to_words = grouped[:, g, :, :].rearrange("p (n i) t -> p n t i", i=RUN)
+                from_rows = raw[c][:, g, :, :].rearrange("p t (n i) -> p n t i", i=RUN)
+                split = VECTOR_SHARE // RUN
+                nc.vector.tensor_copy(out=to_words[:, :split], in_=from_rows[:, :split])
+                nc.scalar.copy(out=to_words[:, split:], in_=from_rows[:, split:])
+
+            def quantise_pass(g):
+                nc.vector.quantize_mx(
+                    out=codes[c][:, g, :].bitcast(FP8X4),
+                    scales=planes[c][:, g, :],
+                    in_=grouped[:, g, :, :].rearrange("p w t -> p (w t)"),
+                )
+
+            regroup(0)
+            for g in range(1, PASSES):
+                regroup(g)
+                quantise_pass(g - 1)
+            quantise_pass(PASSES - 1)
+
+        def project(c):
+            y_ps[c] = [psum_y.tile([P, CHANNELS], F32, name="y_ps") for i in range(POSITION_TILES)]
+            for g in range(PASSES):
+                for i in range(POSITION_TILES):
+                    tile_cols = slice(i * P, (i + 1) * P)
+                    nc.tensor.matmul_mx(
+                        out=y_ps[c][i][:],
+                        lhsT=codes[c][:, g, tile_cols].bitcast(FP8X4),
+                        lhsT_scale=planes[c][:, g, tile_cols],
+                        rhs=w_words[:, g, :].bitcast(FP4X4),
+                        rhs_scale=w_scales[:, g, :],
+                        start=(g == 0),
+                        stop=(g == PASSES - 1),
+                    )
+
+        def add_bias(c):
+            y_sb[c] = work.tile([P, POSITION_TILES, CHANNELS], F32, name="y_sb")
+            sums = work.tile([P, POSITION_TILES], F32, name="sums")
+            for i in range(POSITION_TILES):
+                nc.vector.scalar_tensor_tensor(
+                    out=y_sb[c][:, i, :],
+                    in0=y_ps[c][i][:],
+                    scalar=1.0,
+                    in1=bias[:],
+                    op0=ALU.mult,
+                    op1=ALU.add,
+                    accum_out=sums[:, i : i + 1],
+                )
+            neg_mean[c] = work.tile([P, POSITION_TILES], F32, name="neg_mean")
+            nc.vector.tensor_scalar_mul(out=neg_mean[c][:], in0=sums[:], scalar1=-1.0 / CHANNELS)
+
+        def variance(c):
+            squares = work.tile([P, POSITION_TILES], F32, name="squares")
+            for i in range(POSITION_TILES):
+                unread = scratch.tile([P, CHANNELS], BF16, name="unread")
+                nc.scalar.activation(
+                    out=unread[:],
+                    in_=y_sb[c][:, i, :],
+                    func=ACT.Square,
+                    bias=neg_mean[c][:, i : i + 1],
+                    accum_out=squares[:, i : i + 1],
+                )
+            std = work.tile([P, POSITION_TILES], F32, name="std")
+            nc.scalar.activation(out=std[:], in_=squares[:], func=ACT.Sqrt, bias=eps[:], scale=1.0 / CHANNELS)
+            rstd[c] = work.tile([P, POSITION_TILES], F32, name="rstd")
+            nc.vector.reciprocal(out=rstd[c][:], in_=std[:])
+            shift[c] = work.tile([P, POSITION_TILES], F32, name="shift")
+            nc.vector.tensor_mul(out=shift[c][:], in0=neg_mean[c][:], in1=rstd[c][:])
+
+        def normalise(c):
+            z_sb[c] = work.tile([P, POSITION_TILES, CHANNELS], F32, name="z_sb")
+            for i in range(POSITION_TILES):
+                nc.scalar.activation(
+                    out=z_sb[c][:, i, :],
+                    in_=y_sb[c][:, i, :],
+                    func=ACT.Identity,
+                    bias=shift[c][:, i : i + 1],
+                    scale=rstd[c][:, i : i + 1],
+                )
+
+        def transpose(c):
+            zT_ps[c] = [psum_t.tile([P, CHUNK], F32, name="zT_ps") for ct in range(CHANNEL_TILES)]
+            for ct in range(CHANNEL_TILES):
+                for i in range(POSITION_TILES):
+                    nc.tensor.transpose(
+                        zT_ps[c][ct][:, i * P : (i + 1) * P],
+                        z_sb[c][:, i, ct * P : (ct + 1) * P],
+                        ident_f32[:],
+                    )
+
+        def finish(c):
+            b, cols = image_and_columns(c)
+            result = work.tile([P, CHANNEL_TILES, CHUNK], F32, name="result")
+            for ct in range(CHANNEL_TILES):
+                nc.vector.scalar_tensor_tensor(
+                    out=result[:, ct, :],
+                    in0=zT_ps[c][ct][:],
+                    scalar=gain[:, ct : ct + 1],
+                    in1=xn_sb[b][:, ct, cols],
+                    op0=ALU.mult,
+                    op1=ALU.add,
+                )
+                nc.sync.dma_start(out=out_dram[b, ct * P : (ct + 1) * P, cols], in_=result[:, ct, :])
+
+        quantise(0)
+        project(0)
+        for c in range(CHUNKS):
+            if c >= 1:
+                transpose(c - 1)
+            add_bias(c)
+            if c + 1 < CHUNKS:
+                quantise(c + 1)
+                project(c + 1)
+            variance(c)
+            if c >= 1:
+                finish(c - 1)
+            normalise(c)
+        transpose(CHUNKS - 1)
+        finish(CHUNKS - 1)

@@ -20,6 +20,7 @@ K_PASS = P * PACK
 IMAGES = 2
 K = 1536
 PASSES = K // K_PASS
+UNITS = IMAGES * PASSES
 CHANNELS = 512
 CHANNEL_TILES = CHANNELS // P
 POSITIONS = 1024
@@ -27,7 +28,7 @@ CHUNK = 512
 POSITION_TILES = CHUNK // P
 CHUNKS_PER_IMAGE = POSITIONS // CHUNK
 CHUNKS = IMAGES * CHUNKS_PER_IMAGE
-VECTOR_SHARE = CHUNK // 2
+VECTOR_SHARE = POSITIONS // 2
 RUN = 4
 EPS = 1e-5
 
@@ -42,9 +43,8 @@ def tile_linearattention_pb_kernel(tc, h_attn, xn, Wout_words, Wout_scales, bout
 
     with ExitStack() as ctx:
         consts = ctx.enter_context(tc.tile_pool(name="consts", bufs=1))
-        raw_pool = ctx.enter_context(tc.tile_pool(name="raw", bufs=CHUNKS))
-        xn_pool = ctx.enter_context(tc.tile_pool(name="xn", bufs=IMAGES))
-        work = ctx.enter_context(tc.tile_pool(name="work", bufs=2))
+        per_image = ctx.enter_context(tc.tile_pool(name="per_image", bufs=IMAGES))
+        work = ctx.enter_context(tc.tile_pool(name="work", bufs=3))
         scratch = ctx.enter_context(tc.tile_pool(name="scratch", bufs=POSITION_TILES))
         psum_y = ctx.enter_context(tc.psum_pool(name="psum_y", bufs=POSITION_TILES))
         psum_t = ctx.enter_context(tc.psum_pool(name="psum_t", bufs=CHANNEL_TILES))
@@ -72,27 +72,21 @@ def tile_linearattention_pb_kernel(tc, h_attn, xn, Wout_words, Wout_scales, bout
         raw = []
         xn_sb = []
 
-        def image_and_columns(c):
-            first = (c % CHUNKS_PER_IMAGE) * CHUNK
-            return c // CHUNKS_PER_IMAGE, slice(first, first + CHUNK)
-
-        def load_chunk(c):
-            b, cols = image_and_columns(c)
-            raw_c = raw_pool.tile([P, PASSES, PACK, CHUNK], BF16, name="raw_c")
+        def load_image(b):
+            raw_b = per_image.tile([P, PASSES, PACK, POSITIONS], BF16, name="raw_b")
             for g in range(PASSES):
                 k_rows = slice(g * K_PASS, (g + 1) * K_PASS)
                 nc.sync.dma_start(
-                    out=raw_c[:, g, :, :],
-                    in_=h_dram[b, k_rows, cols].rearrange("(p t) w -> p t w", t=PACK),
+                    out=raw_b[:, g, :, :], in_=h_dram[b, k_rows, :].rearrange("(p t) w -> p t w", t=PACK)
                 )
-            raw.append(raw_c)
+            raw.append(raw_b)
 
         def load_residual(b):
-            xn_b = xn_pool.tile([P, CHANNEL_TILES, POSITIONS], BF16, name="xn_b")
+            xn_b = per_image.tile([P, CHANNEL_TILES, POSITIONS], BF16, name="xn_b")
             nc.sync.dma_start(out=xn_b[:], in_=xn_dram[b].rearrange("(ct p) w -> p ct w", p=P))
             xn_sb.append(xn_b)
 
-        load_chunk(0)
+        load_image(0)
 
         w_words = consts.tile([P, PASSES, 2 * CHANNELS], U8, align_bytes=64)
         nc.sync.dma_start(
@@ -108,10 +102,8 @@ def tile_linearattention_pb_kernel(tc, h_attn, xn, Wout_words, Wout_scales, bout
                 .rearrange("g r n -> r g n"),
             )
 
-        load_chunk(1)
+        load_image(1)
         load_residual(0)
-        load_chunk(2)
-        load_chunk(3)
         load_residual(1)
 
         bias_ps = psum_y.tile([P, CHANNELS], F32, name="y_ps")
@@ -123,43 +115,44 @@ def tile_linearattention_pb_kernel(tc, h_attn, xn, Wout_words, Wout_scales, bout
         gain = consts.tile([P, CHANNEL_TILES], F32)
         nc.vector.tensor_copy(out=gain[:], in_=gain_ps[:, 0:CHANNEL_TILES])
 
-        codes, planes, y_ps, y_sb, z_sb, zT_ps = {}, {}, {}, {}, {}, {}
-        neg_mean, rstd, shift = {}, {}, {}
+        codes = [per_image.tile([P, PASSES, POSITIONS], U32, name="codes", align_bytes=64) for b in range(IMAGES)]
+        planes = [per_image.tile([P, PASSES, POSITIONS], U8, name="planes", align_bytes=64) for b in range(IMAGES)]
+        grouped = {}
 
-        def quantise(c):
-            grouped = work.tile([P, PASSES, CHUNK, PACK], BF16, name="grouped", align_bytes=64)
-            codes[c] = work.tile([P, PASSES, CHUNK], U32, name="codes", align_bytes=64)
-            planes[c] = work.tile([P, PASSES, CHUNK], U8, name="planes", align_bytes=64)
+        def regroup(unit):
+            b, g = divmod(unit, PASSES)
+            grouped[unit] = work.tile([P, POSITIONS, PACK], BF16, name="grouped", align_bytes=64)
+            to_words = grouped[unit][:].rearrange("p (n i) t -> p n t i", i=RUN)
+            from_rows = raw[b][:, g, :, :].rearrange("p t (n i) -> p n t i", i=RUN)
+            split = VECTOR_SHARE // RUN
+            nc.vector.tensor_copy(out=to_words[:, :split], in_=from_rows[:, :split])
+            nc.scalar.copy(out=to_words[:, split:], in_=from_rows[:, split:])
 
-            def regroup(g):
-                to_words = grouped[:, g, :, :].rearrange("p (n i) t -> p n t i", i=RUN)
-                from_rows = raw[c][:, g, :, :].rearrange("p t (n i) -> p n t i", i=RUN)
-                split = VECTOR_SHARE // RUN
-                nc.vector.tensor_copy(out=to_words[:, :split], in_=from_rows[:, :split])
-                nc.scalar.copy(out=to_words[:, split:], in_=from_rows[:, split:])
+        def quantise(unit):
+            b, g = divmod(unit, PASSES)
+            nc.vector.quantize_mx(
+                out=codes[b][:, g, :].bitcast(FP8X4),
+                scales=planes[b][:, g, :],
+                in_=grouped[unit][:].rearrange("p w t -> p (w t)"),
+            )
 
-            def quantise_pass(g):
-                nc.vector.quantize_mx(
-                    out=codes[c][:, g, :].bitcast(FP8X4),
-                    scales=planes[c][:, g, :],
-                    in_=grouped[:, g, :, :].rearrange("p w t -> p (w t)"),
-                )
+        y_ps, y_sb, z_sb, zT_ps = {}, {}, {}, {}
+        sums, squares, std, rstd, shift = {}, {}, {}, {}, {}
 
-            regroup(0)
-            for g in range(1, PASSES):
-                regroup(g)
-                quantise_pass(g - 1)
-            quantise_pass(PASSES - 1)
+        def image_and_columns(c):
+            first = (c % CHUNKS_PER_IMAGE) * CHUNK
+            return c // CHUNKS_PER_IMAGE, first
 
         def project(c):
+            b, first = image_and_columns(c)
             y_ps[c] = [psum_y.tile([P, CHANNELS], F32, name="y_ps") for i in range(POSITION_TILES)]
-            for g in range(PASSES):
-                for i in range(POSITION_TILES):
-                    tile_cols = slice(i * P, (i + 1) * P)
+            for i in range(POSITION_TILES):
+                tile_cols = slice(first + i * P, first + (i + 1) * P)
+                for g in range(PASSES):
                     nc.tensor.matmul_mx(
                         out=y_ps[c][i][:],
-                        lhsT=codes[c][:, g, tile_cols].bitcast(FP8X4),
-                        lhsT_scale=planes[c][:, g, tile_cols],
+                        lhsT=codes[b][:, g, tile_cols].bitcast(FP8X4),
+                        lhsT_scale=planes[b][:, g, tile_cols],
                         rhs=w_words[:, g, :].bitcast(FP4X4),
                         rhs_scale=w_scales[:, g, :],
                         start=(g == 0),
@@ -168,7 +161,7 @@ def tile_linearattention_pb_kernel(tc, h_attn, xn, Wout_words, Wout_scales, bout
 
         def add_bias(c):
             y_sb[c] = work.tile([P, POSITION_TILES, CHANNELS], F32, name="y_sb")
-            sums = work.tile([P, POSITION_TILES], F32, name="sums")
+            sums[c] = work.tile([P, POSITION_TILES], F32, name="sums")
             for i in range(POSITION_TILES):
                 nc.vector.scalar_tensor_tensor(
                     out=y_sb[c][:, i, :],
@@ -177,39 +170,61 @@ def tile_linearattention_pb_kernel(tc, h_attn, xn, Wout_words, Wout_scales, bout
                     in1=bias[:],
                     op0=ALU.mult,
                     op1=ALU.add,
-                    accum_out=sums[:, i : i + 1],
+                    accum_out=sums[c][:, i : i + 1],
                 )
-            neg_mean[c] = work.tile([P, POSITION_TILES], F32, name="neg_mean")
-            nc.vector.tensor_scalar_mul(out=neg_mean[c][:], in0=sums[:], scalar1=-1.0 / CHANNELS)
 
-        def variance(c):
-            squares = work.tile([P, POSITION_TILES], F32, name="squares")
+        def sum_squares(c):
+            squares[c] = work.tile([P, POSITION_TILES], F32, name="squares")
             for i in range(POSITION_TILES):
                 unread = scratch.tile([P, CHANNELS], BF16, name="unread")
                 nc.scalar.activation(
                     out=unread[:],
                     in_=y_sb[c][:, i, :],
                     func=ACT.Square,
-                    bias=neg_mean[c][:, i : i + 1],
-                    accum_out=squares[:, i : i + 1],
+                    bias=sums[c][:, i : i + 1],
+                    scale=-1.0 * CHANNELS,
+                    accum_out=squares[c][:, i : i + 1],
                 )
-            std = work.tile([P, POSITION_TILES], F32, name="std")
-            nc.scalar.activation(out=std[:], in_=squares[:], func=ACT.Sqrt, bias=eps[:], scale=1.0 / CHANNELS)
+
+        def standard_deviation(c):
+            std[c] = work.tile([P, POSITION_TILES], F32, name="std")
+            nc.scalar.activation(
+                out=std[c][:], in_=squares[c][:], func=ACT.Sqrt, bias=eps[:], scale=1.0 / CHANNELS**3
+            )
+
+        def scale_and_shift(c):
             rstd[c] = work.tile([P, POSITION_TILES], F32, name="rstd")
-            nc.vector.reciprocal(out=rstd[c][:], in_=std[:])
+            nc.vector.reciprocal(out=rstd[c][:], in_=std[c][:])
             shift[c] = work.tile([P, POSITION_TILES], F32, name="shift")
-            nc.vector.tensor_mul(out=shift[c][:], in0=neg_mean[c][:], in1=rstd[c][:])
+            nc.vector.scalar_tensor_tensor(
+                out=shift[c][:],
+                in0=sums[c][:],
+                scalar=-1.0 / CHANNELS,
+                in1=rstd[c][:],
+                op0=ALU.mult,
+                op1=ALU.mult,
+            )
 
         def normalise(c):
             z_sb[c] = work.tile([P, POSITION_TILES, CHANNELS], F32, name="z_sb")
             for i in range(POSITION_TILES):
-                nc.scalar.activation(
-                    out=z_sb[c][:, i, :],
-                    in_=y_sb[c][:, i, :],
-                    func=ACT.Identity,
-                    bias=shift[c][:, i : i + 1],
-                    scale=rstd[c][:, i : i + 1],
-                )
+                if i % 2 == 0:
+                    nc.gpsimd.tensor_scalar(
+                        out=z_sb[c][:, i, :],
+                        in0=y_sb[c][:, i, :],
+                        scalar1=rstd[c][:, i : i + 1],
+                        scalar2=shift[c][:, i : i + 1],
+                        op0=ALU.mult,
+                        op1=ALU.add,
+                    )
+                else:
+                    nc.scalar.activation(
+                        out=z_sb[c][:, i, :],
+                        in_=y_sb[c][:, i, :],
+                        func=ACT.Identity,
+                        bias=shift[c][:, i : i + 1],
+                        scale=rstd[c][:, i : i + 1],
+                    )
 
         def transpose(c):
             zT_ps[c] = [psum_t.tile([P, CHUNK], F32, name="zT_ps") for ct in range(CHANNEL_TILES)]
@@ -222,7 +237,8 @@ def tile_linearattention_pb_kernel(tc, h_attn, xn, Wout_words, Wout_scales, bout
                     )
 
         def finish(c):
-            b, cols = image_and_columns(c)
+            b, first = image_and_columns(c)
+            cols = slice(first, first + CHUNK)
             result = work.tile([P, CHANNEL_TILES, CHUNK], F32, name="result")
             for ct in range(CHANNEL_TILES):
                 nc.vector.scalar_tensor_tensor(
@@ -235,18 +251,28 @@ def tile_linearattention_pb_kernel(tc, h_attn, xn, Wout_words, Wout_scales, bout
                 )
                 nc.sync.dma_start(out=out_dram[b, ct * P : (ct + 1) * P, cols], in_=result[:, ct, :])
 
-        quantise(0)
+        regroup(0)
+        for unit in range(1, PASSES + 1):
+            regroup(unit)
+            quantise(unit - 1)
         project(0)
-        for c in range(CHUNKS):
-            if c >= 1:
-                transpose(c - 1)
-            add_bias(c)
-            if c + 1 < CHUNKS:
-                quantise(c + 1)
-                project(c + 1)
-            variance(c)
-            if c >= 1:
-                finish(c - 1)
-            normalise(c)
-        transpose(CHUNKS - 1)
-        finish(CHUNKS - 1)
+        for step in range(CHUNKS + 2):
+            if 1 <= step <= CHUNKS:
+                standard_deviation(step - 1)
+            if step >= 2:
+                transpose(step - 2)
+            if step < CHUNKS:
+                add_bias(step)
+                sum_squares(step)
+            if step + 1 < CHUNKS:
+                project(step + 1)
+            if step == 0:
+                for unit in range(PASSES + 1, UNITS):
+                    regroup(unit)
+                    quantise(unit - 1)
+                quantise(UNITS - 1)
+            if 1 <= step <= CHUNKS:
+                scale_and_shift(step - 1)
+                normalise(step - 1)
+            if step >= 2:
+                finish(step - 2)

@@ -48,7 +48,6 @@ def tile_linearattention_pb_kernel(tc, h_attn, xn, Wout_words, Wout_scales, bout
         scratch = ctx.enter_context(tc.tile_pool(name="scratch", bufs=POSITION_TILES))
         psum_y = ctx.enter_context(tc.psum_pool(name="psum_y", bufs=POSITION_TILES))
         psum_t = ctx.enter_context(tc.psum_pool(name="psum_t", bufs=CHANNEL_TILES))
-        ctx.enter_context(tc.manual_schedule())
 
         ident_f32 = consts.tile([P, P], F32)
         make_identity(nc, ident_f32[:])

@@ -28,7 +28,8 @@ CHUNK = 512
 POSITION_TILES = CHUNK // P
 CHUNKS_PER_IMAGE = POSITIONS // CHUNK
 CHUNKS = IMAGES * CHUNKS_PER_IMAGE
-VECTOR_SHARE = POSITIONS // 2
+VECTOR_SHARE = POSITIONS // 4
+GPSIMD_SHARE = POSITIONS // 4
 RUN = 4
 EPS = 1e-5
 
@@ -123,9 +124,20 @@ def tile_linearattention_pb_kernel(tc, h_attn, xn, Wout_words, Wout_scales, bout
             grouped[unit] = work.tile([P, POSITIONS, PACK], BF16, name="grouped", align_bytes=64)
             to_words = grouped[unit][:].rearrange("p (n i) t -> p n t i", i=RUN)
             from_rows = raw[b][:, g, :, :].rearrange("p t (n i) -> p n t i", i=RUN)
-            split = VECTOR_SHARE // RUN
-            nc.vector.tensor_copy(out=to_words[:, :split], in_=from_rows[:, :split])
-            nc.scalar.copy(out=to_words[:, split:], in_=from_rows[:, split:])
+            gpsimd_cols = slice(VECTOR_SHARE, VECTOR_SHARE + GPSIMD_SHARE)
+            nc.vector.tensor_copy(
+                out=to_words[:, : VECTOR_SHARE // RUN], in_=from_rows[:, : VECTOR_SHARE // RUN]
+            )
+            nc.gpsimd.tensor_scalar(
+                out=grouped[unit][:, gpsimd_cols, :],
+                in0=raw[b][:, g, :, gpsimd_cols].rearrange("p t w -> p w t"),
+                scalar1=1.0,
+                scalar2=0.0,
+                op0=ALU.mult,
+                op1=ALU.add,
+            )
+            scalar_from = (VECTOR_SHARE + GPSIMD_SHARE) // RUN
+            nc.scalar.copy(out=to_words[:, scalar_from:], in_=from_rows[:, scalar_from:])
 
         def quantise(unit):
             b, g = divmod(unit, PASSES)
@@ -207,7 +219,7 @@ def tile_linearattention_pb_kernel(tc, h_attn, xn, Wout_words, Wout_scales, bout
         def normalise(c):
             z_sb[c] = work.tile([P, POSITION_TILES, CHANNELS], F32, name="z_sb")
             for i in range(POSITION_TILES):
-                if i % 2 == 0:
+                if i < POSITION_TILES - 1:
                     nc.gpsimd.tensor_scalar(
                         out=z_sb[c][:, i, :],
                         in0=y_sb[c][:, i, :],

@@ -20,7 +20,6 @@ K_PASS = P * PACK
 IMAGES = 2
 K = 1536
 PASSES = K // K_PASS
-UNITS = IMAGES * PASSES
 CHANNELS = 512
 CHANNEL_TILES = CHANNELS // P
 POSITIONS = 1024
@@ -28,8 +27,7 @@ CHUNK = 512
 POSITION_TILES = CHUNK // P
 CHUNKS_PER_IMAGE = POSITIONS // CHUNK
 CHUNKS = IMAGES * CHUNKS_PER_IMAGE
-VECTOR_SHARE = POSITIONS // 4
-GPSIMD_SHARE = POSITIONS // 4
+VECTOR_SHARE = CHUNK // 2
 RUN = 4
 EPS = 1e-5
 
@@ -45,6 +43,7 @@ def tile_linearattention_pb_kernel(tc, h_attn, xn, Wout_words, Wout_scales, bout
     with ExitStack() as ctx:
         consts = ctx.enter_context(tc.tile_pool(name="consts", bufs=1))
         per_image = ctx.enter_context(tc.tile_pool(name="per_image", bufs=IMAGES))
+        per_chunk = ctx.enter_context(tc.tile_pool(name="per_chunk", bufs=CHUNKS))
         work = ctx.enter_context(tc.tile_pool(name="work", bufs=3))
         scratch = ctx.enter_context(tc.tile_pool(name="scratch", bufs=POSITION_TILES))
         psum_y = ctx.enter_context(tc.psum_pool(name="psum_y", bufs=POSITION_TILES))
@@ -72,21 +71,26 @@ def tile_linearattention_pb_kernel(tc, h_attn, xn, Wout_words, Wout_scales, bout
         raw = []
         xn_sb = []
 
-        def load_image(b):
-            raw_b = per_image.tile([P, PASSES, PACK, POSITIONS], BF16, name="raw_b")
+        def image_and_columns(c):
+            first = (c % CHUNKS_PER_IMAGE) * CHUNK
+            return c // CHUNKS_PER_IMAGE, slice(first, first + CHUNK)
+
+        def load_chunk(c):
+            b, cols = image_and_columns(c)
+            raw_c = per_chunk.tile([P, PASSES, PACK, CHUNK], BF16, name="raw_c")
             for g in range(PASSES):
                 k_rows = slice(g * K_PASS, (g + 1) * K_PASS)
                 nc.sync.dma_start(
-                    out=raw_b[:, g, :, :], in_=h_dram[b, k_rows, :].rearrange("(p t) w -> p t w", t=PACK)
+                    out=raw_c[:, g, :, :], in_=h_dram[b, k_rows, cols].rearrange("(p t) w -> p t w", t=PACK)
                 )
-            raw.append(raw_b)
+            raw.append(raw_c)
 
         def load_residual(b):
             xn_b = per_image.tile([P, CHANNEL_TILES, POSITIONS], BF16, name="xn_b")
             nc.sync.dma_start(out=xn_b[:], in_=xn_dram[b].rearrange("(ct p) w -> p ct w", p=P))
             xn_sb.append(xn_b)
 
-        load_image(0)
+        load_chunk(0)
 
         w_words = consts.tile([P, PASSES, 2 * CHANNELS], U8, align_bytes=64)
         nc.sync.dma_start(
@@ -102,8 +106,10 @@ def tile_linearattention_pb_kernel(tc, h_attn, xn, Wout_words, Wout_scales, bout
                 .rearrange("g r n -> r g n"),
             )
 
-        load_image(1)
+        load_chunk(1)
         load_residual(0)
+        load_chunk(2)
+        load_chunk(3)
         load_residual(1)
 
         bias_ps = psum_y.tile([P, CHANNELS], F32, name="y_ps")
@@ -115,55 +121,44 @@ def tile_linearattention_pb_kernel(tc, h_attn, xn, Wout_words, Wout_scales, bout
         gain = consts.tile([P, CHANNEL_TILES], F32)
         nc.vector.tensor_copy(out=gain[:], in_=gain_ps[:, 0:CHANNEL_TILES])
 
-        codes = [per_image.tile([P, PASSES, POSITIONS], U32, name="codes", align_bytes=64) for b in range(IMAGES)]
-        planes = [per_image.tile([P, PASSES, POSITIONS], U8, name="planes", align_bytes=64) for b in range(IMAGES)]
+        codes = [per_chunk.tile([P, PASSES, CHUNK], U32, name="codes", align_bytes=64) for c in range(CHUNKS)]
+        planes = [per_chunk.tile([P, PASSES, CHUNK], U8, name="planes", align_bytes=64) for c in range(CHUNKS)]
         grouped = {}
 
-        def regroup(unit):
-            b, g = divmod(unit, PASSES)
-            grouped[unit] = work.tile([P, POSITIONS, PACK], BF16, name="grouped", align_bytes=64)
-            to_words = grouped[unit][:].rearrange("p (n i) t -> p n t i", i=RUN)
-            from_rows = raw[b][:, g, :, :].rearrange("p t (n i) -> p n t i", i=RUN)
-            gpsimd_cols = slice(VECTOR_SHARE, VECTOR_SHARE + GPSIMD_SHARE)
-            nc.vector.tensor_copy(
-                out=to_words[:, : VECTOR_SHARE // RUN], in_=from_rows[:, : VECTOR_SHARE // RUN]
-            )
-            nc.gpsimd.tensor_scalar(
-                out=grouped[unit][:, gpsimd_cols, :],
-                in0=raw[b][:, g, :, gpsimd_cols].rearrange("p t w -> p w t"),
-                scalar1=1.0,
-                scalar2=0.0,
-                op0=ALU.mult,
-                op1=ALU.add,
-            )
-            scalar_from = (VECTOR_SHARE + GPSIMD_SHARE) // RUN
-            nc.scalar.copy(out=to_words[:, scalar_from:], in_=from_rows[:, scalar_from:])
+        def regroup(c, g):
+            grouped[c, g] = work.tile([P, CHUNK, PACK], BF16, name="grouped", align_bytes=64)
+            to_words = grouped[c, g][:].rearrange("p (n i) t -> p n t i", i=RUN)
+            from_rows = raw[c][:, g, :, :].rearrange("p t (n i) -> p n t i", i=RUN)
+            split = VECTOR_SHARE // RUN
+            nc.vector.tensor_copy(out=to_words[:, :split], in_=from_rows[:, :split])
+            nc.scalar.copy(out=to_words[:, split:], in_=from_rows[:, split:])
 
-        def quantise(unit):
-            b, g = divmod(unit, PASSES)
+        def quantise(c, g):
             nc.vector.quantize_mx(
-                out=codes[b][:, g, :].bitcast(FP8X4),
-                scales=planes[b][:, g, :],
-                in_=grouped[unit][:].rearrange("p w t -> p (w t)"),
+                out=codes[c][:, g, :].bitcast(FP8X4),
+                scales=planes[c][:, g, :],
+                in_=grouped[c, g][:].rearrange("p w t -> p (w t)"),
             )
+
+        def prepare(c):
+            regroup(c, 0)
+            for g in range(1, PASSES):
+                regroup(c, g)
+                quantise(c, g - 1)
+            quantise(c, PASSES - 1)
 
         y_ps, y_sb, z_sb, zT_ps = {}, {}, {}, {}
         sums, squares, std, rstd, shift = {}, {}, {}, {}, {}
 
-        def image_and_columns(c):
-            first = (c % CHUNKS_PER_IMAGE) * CHUNK
-            return c // CHUNKS_PER_IMAGE, first
-
         def project(c):
-            b, first = image_and_columns(c)
             y_ps[c] = [psum_y.tile([P, CHANNELS], F32, name="y_ps") for i in range(POSITION_TILES)]
             for i in range(POSITION_TILES):
-                tile_cols = slice(first + i * P, first + (i + 1) * P)
+                tile_cols = slice(i * P, (i + 1) * P)
                 for g in range(PASSES):
                     nc.tensor.matmul_mx(
                         out=y_ps[c][i][:],
-                        lhsT=codes[b][:, g, tile_cols].bitcast(FP8X4),
-                        lhsT_scale=planes[b][:, g, tile_cols],
+                        lhsT=codes[c][:, g, tile_cols].bitcast(FP8X4),
+                        lhsT_scale=planes[c][:, g, tile_cols],
                         rhs=w_words[:, g, :].bitcast(FP4X4),
                         rhs_scale=w_scales[:, g, :],
                         start=(g == 0),
@@ -219,7 +214,7 @@ def tile_linearattention_pb_kernel(tc, h_attn, xn, Wout_words, Wout_scales, bout
         def normalise(c):
             z_sb[c] = work.tile([P, POSITION_TILES, CHANNELS], F32, name="z_sb")
             for i in range(POSITION_TILES):
-                if i < POSITION_TILES - 1:
+                if i % 2 == 0:
                     nc.gpsimd.tensor_scalar(
                         out=z_sb[c][:, i, :],
                         in0=y_sb[c][:, i, :],
@@ -248,8 +243,7 @@ def tile_linearattention_pb_kernel(tc, h_attn, xn, Wout_words, Wout_scales, bout
                     )
 
         def finish(c):
-            b, first = image_and_columns(c)
-            cols = slice(first, first + CHUNK)
+            b, cols = image_and_columns(c)
             result = work.tile([P, CHANNEL_TILES, CHUNK], F32, name="result")
             for ct in range(CHANNEL_TILES):
                 nc.vector.scalar_tensor_tensor(
@@ -262,11 +256,9 @@ def tile_linearattention_pb_kernel(tc, h_attn, xn, Wout_words, Wout_scales, bout
                 )
                 nc.sync.dma_start(out=out_dram[b, ct * P : (ct + 1) * P, cols], in_=result[:, ct, :])
 
-        regroup(0)
-        for unit in range(1, PASSES + 1):
-            regroup(unit)
-            quantise(unit - 1)
+        prepare(0)
         project(0)
+        prepare(1)
         for step in range(CHUNKS + 2):
             if 1 <= step <= CHUNKS:
                 standard_deviation(step - 1)
@@ -277,11 +269,8 @@ def tile_linearattention_pb_kernel(tc, h_attn, xn, Wout_words, Wout_scales, bout
                 sum_squares(step)
             if step + 1 < CHUNKS:
                 project(step + 1)
-            if step == 0:
-                for unit in range(PASSES + 1, UNITS):
-                    regroup(unit)
-                    quantise(unit - 1)
-                quantise(UNITS - 1)
+            if step + 2 < CHUNKS:
+                prepare(step + 2)
             if 1 <= step <= CHUNKS:
                 scale_and_shift(step - 1)
                 normalise(step - 1)

@@ -107,9 +107,9 @@ def tile_linearattention_pb_kernel(tc, h_attn, xn, Wout_words, Wout_scales, bout
             )
 
         load_chunk(1)
-        load_residual(0)
         load_chunk(2)
         load_chunk(3)
+        load_residual(0)
         load_residual(1)
 
         bias_ps = psum_y.tile([P, CHANNELS], F32, name="y_ps")

@@ -58,7 +58,7 @@ def tile_linearattention_pb_kernel(tc, h_attn, xn, Wout_words, Wout_scales, bout
         eps = consts.tile([P, 1], F32)
         nc.vector.memset(eps[:], EPS)
         warm = consts.tile([P, 1], F32)
-        nc.scalar.activation(out=warm[:], in_=eps[:], func=ACT.Sqrt)
+        nc.scalar.activation(out=warm[:], in_=eps[:], func=ACT.Abs_reciprocal_sqrt)
 
         rows = consts.tile([P, CHANNELS + P], BF16)
         nc.vector.memset(rows[:], 0.0)
@@ -193,23 +193,22 @@ def tile_linearattention_pb_kernel(tc, h_attn, xn, Wout_words, Wout_scales, bout
                 )
 
         def standard_deviation(c):
-            std[c] = work.tile([P, POSITION_TILES], F32, name="std")
+            rstd[c] = work.tile([P, POSITION_TILES], F32, name="rstd")
             nc.scalar.activation(
-                out=std[c][:], in_=squares[c][:], func=ACT.Sqrt, bias=eps[:], scale=1.0 / CHANNELS**3
+                out=rstd[c][:],
+                in_=squares[c][:],
+                func=ACT.Abs_reciprocal_sqrt,
+                bias=eps[:],
+                scale=1.0 / CHANNELS**3,
             )
 
         def scale_and_shift(c):
-            rstd[c] = work.tile([P, POSITION_TILES], F32, name="rstd")
-            nc.vector.reciprocal(out=rstd[c][:], in_=std[c][:])
-            shift[c] = work.tile([P, POSITION_TILES], F32, name="shift")
-            nc.vector.scalar_tensor_tensor(
-                out=shift[c][:],
-                in0=sums[c][:],
-                scalar=-1.0 / CHANNELS,
-                in1=rstd[c][:],
-                op0=ALU.mult,
-                op1=ALU.mult,
+            std[c] = work.tile([P, POSITION_TILES], F32, name="std")
+            nc.gpsimd.tensor_scalar(
+                out=std[c][:], in0=sums[c][:], scalar1=-1.0 / CHANNELS, scalar2=0.0, op0=ALU.mult, op1=ALU.add
             )
+            shift[c] = work.tile([P, POSITION_TILES], F32, name="shift")
+            nc.gpsimd.tensor_tensor(out=shift[c][:], in0=std[c][:], in1=rstd[c][:], op=ALU.mult)
 
         def normalise(c):
             z_sb[c] = work.tile([P, POSITION_TILES, CHANNELS], F32, name="z_sb")

@@ -62,11 +62,6 @@ def tile_linearattention_pb_kernel(tc, h_attn, xn, Wout_words, Wout_scales, bout
 
         rows = consts.tile([P, CHANNELS + P], BF16)
         nc.vector.memset(rows[:], 0.0)
-        nc.sync.dma_start(out=rows[0:1, 0:CHANNELS], in_=bout.rearrange("(o c) -> o c", o=1))
-        nc.sync.dma_start(
-            out=rows[0:CHANNEL_TILES, CHANNELS:],
-            in_=outnorm_g.rearrange("o (t p) h w -> (o t) (p h w)", p=P),
-        )
 
         raw = []
         xn_sb = []
@@ -91,6 +86,11 @@ def tile_linearattention_pb_kernel(tc, h_attn, xn, Wout_words, Wout_scales, bout
             xn_sb.append(xn_b)
 
         load_chunk(0)
+        nc.sync.dma_start(out=rows[0:1, 0:CHANNELS], in_=bout.rearrange("(o c) -> o c", o=1))
+        nc.sync.dma_start(
+            out=rows[0:CHANNEL_TILES, CHANNELS:],
+            in_=outnorm_g.rearrange("o (t p) h w -> (o t) (p h w)", p=P),
+        )
 
         w_words = consts.tile([P, PASSES, 2 * CHANNELS], U8, align_bytes=64)
         nc.sync.dma_start(

@@ -214,7 +214,8 @@ def tile_linearattention_pb_kernel(tc, h_attn, xn, Wout_words, Wout_scales, bout
             z_sb[c] = work.tile([P, POSITION_TILES, CHANNELS], F32, name="z_sb")
             for i in range(POSITION_TILES):
                 if i % 2 == 0:
-                    nc.gpsimd.tensor_scalar(
+                    engine = nc.vector if c == 0 else nc.gpsimd
+                    engine.tensor_scalar(
                         out=z_sb[c][:, i, :],
                         in0=y_sb[c][:, i, :],
                         scalar1=rstd[c][:, i : i + 1],

@@ -27,7 +27,7 @@ CHUNK = 512
 POSITION_TILES = CHUNK // P
 CHUNKS_PER_IMAGE = POSITIONS // CHUNK
 CHUNKS = IMAGES * CHUNKS_PER_IMAGE
-VECTOR_SHARE = CHUNK // 2
+VECTOR_SHARE = 208
 RUN = 4
 EPS = 1e-5
 
@@ -45,6 +45,7 @@ def tile_linearattention_pb_kernel(tc, h_attn, xn, Wout_words, Wout_scales, bout
         per_image = ctx.enter_context(tc.tile_pool(name="per_image", bufs=IMAGES))
         per_chunk = ctx.enter_context(tc.tile_pool(name="per_chunk", bufs=CHUNKS))
         work = ctx.enter_context(tc.tile_pool(name="work", bufs=3))
+        staging = ctx.enter_context(tc.tile_pool(name="staging", bufs=2 * PASSES))
         scratch = ctx.enter_context(tc.tile_pool(name="scratch", bufs=POSITION_TILES))
         psum_y = ctx.enter_context(tc.psum_pool(name="psum_y", bufs=POSITION_TILES))
         psum_t = ctx.enter_context(tc.psum_pool(name="psum_t", bufs=CHANNEL_TILES))
@@ -126,12 +127,13 @@ def tile_linearattention_pb_kernel(tc, h_attn, xn, Wout_words, Wout_scales, bout
         grouped = {}
 
         def regroup(c, g):
-            grouped[c, g] = work.tile([P, CHUNK, PACK], BF16, name="grouped", align_bytes=64)
+            grouped[c, g] = staging.tile([P, CHUNK, PACK], BF16, name="grouped", align_bytes=64)
             to_words = grouped[c, g][:].rearrange("p (n i) t -> p n t i", i=RUN)
             from_rows = raw[c][:, g, :, :].rearrange("p t (n i) -> p n t i", i=RUN)
             split = VECTOR_SHARE // RUN
             nc.vector.tensor_copy(out=to_words[:, :split], in_=from_rows[:, :split])
-            nc.scalar.copy(out=to_words[:, split:], in_=from_rows[:, split:])
+            with tc.high_priority(offset=10000):
+                nc.scalar.copy(out=to_words[:, split:], in_=from_rows[:, split:])
 
         def quantise(c, g):
             nc.vector.quantize_mx(
@@ -213,9 +215,8 @@ def tile_linearattention_pb_kernel(tc, h_attn, xn, Wout_words, Wout_scales, bout
         def normalise(c):
             z_sb[c] = work.tile([P, POSITION_TILES, CHANNELS], F32, name="z_sb")
             for i in range(POSITION_TILES):
-                if i % 2 == 0:
-                    engine = nc.vector if c == 0 else nc.gpsimd
-                    engine.tensor_scalar(
+                if i < POSITION_TILES - 1:
+                    nc.gpsimd.tensor_scalar(
                         out=z_sb[c][:, i, :],
                         in0=y_sb[c][:, i, :],
                         scalar1=rstd[c][:, i : i + 1],

@@ -27,7 +27,7 @@ CHUNK = 512
 POSITION_TILES = CHUNK // P
 CHUNKS_PER_IMAGE = POSITIONS // CHUNK
 CHUNKS = IMAGES * CHUNKS_PER_IMAGE
-VECTOR_SHARE = 208
+VECTOR_SHARES = (272, 224, 192, 160)
 RUN = 4
 EPS = 1e-5
 
@@ -46,14 +46,13 @@ def tile_linearattention_pb_kernel(tc, h_attn, xn, Wout_words, Wout_scales, bout
         per_chunk = ctx.enter_context(tc.tile_pool(name="per_chunk", bufs=CHUNKS))
         work = ctx.enter_context(tc.tile_pool(name="work", bufs=3))
         staging = ctx.enter_context(tc.tile_pool(name="staging", bufs=2 * PASSES))
+        stats = ctx.enter_context(tc.tile_pool(name="stats", bufs=CHUNKS))
         scratch = ctx.enter_context(tc.tile_pool(name="scratch", bufs=POSITION_TILES))
         psum_y = ctx.enter_context(tc.psum_pool(name="psum_y", bufs=POSITION_TILES))
         psum_t = ctx.enter_context(tc.psum_pool(name="psum_t", bufs=CHANNEL_TILES))
 
         ident_f32 = consts.tile([P, P], F32)
         make_identity(nc, ident_f32[:])
-        ident_bf16 = consts.tile([P, P], BF16)
-        make_identity(nc, ident_bf16[:])
         ones = consts.tile([P, P], BF16)
         nc.vector.memset(ones[:], 1.0)
         eps = consts.tile([P, 1], F32)
@@ -61,7 +60,7 @@ def tile_linearattention_pb_kernel(tc, h_attn, xn, Wout_words, Wout_scales, bout
         warm = consts.tile([P, 1], F32)
         nc.scalar.activation(out=warm[:], in_=eps[:], func=ACT.Abs_reciprocal_sqrt)
 
-        rows = consts.tile([P, CHANNELS + P], BF16)
+        rows = consts.tile([P, CHANNELS], BF16)
         nc.vector.memset(rows[:], 0.0)
 
         raw = []
@@ -87,11 +86,7 @@ def tile_linearattention_pb_kernel(tc, h_attn, xn, Wout_words, Wout_scales, bout
             xn_sb.append(xn_b)
 
         load_chunk(0)
-        nc.sync.dma_start(out=rows[0:1, 0:CHANNELS], in_=bout.rearrange("(o c) -> o c", o=1))
-        nc.sync.dma_start(
-            out=rows[0:CHANNEL_TILES, CHANNELS:],
-            in_=outnorm_g.rearrange("o (t p) h w -> (o t) (p h w)", p=P),
-        )
+        nc.sync.dma_start(out=rows[0:1, :], in_=bout.rearrange("(o c) -> o c", o=1))
 
         w_words = consts.tile([P, PASSES, 2 * CHANNELS], U8, align_bytes=64)
         nc.sync.dma_start(
@@ -110,17 +105,17 @@ def tile_linearattention_pb_kernel(tc, h_attn, xn, Wout_words, Wout_scales, bout
         load_chunk(1)
         load_chunk(2)
         load_chunk(3)
+        gain = consts.tile([P, CHANNEL_TILES], BF16)
+        nc.sync.dma_start(out=gain[:], in_=outnorm_g.rearrange("o (ct p) h w -> p (o ct h w)", p=P))
         load_residual(0)
         load_residual(1)
 
-        bias_ps = psum_y.tile([P, CHANNELS], F32, name="y_ps")
-        nc.tensor.matmul(bias_ps[:], lhsT=ones[:], rhs=rows[:, 0:CHANNELS], start=True, stop=True)
         bias = consts.tile([P, CHANNELS], F32)
-        nc.vector.tensor_copy(out=bias[:], in_=bias_ps[:])
-        gain_ps = psum_t.tile([P, P], BF16, name="zT_ps")
-        nc.tensor.transpose(gain_ps[:], rows[:, CHANNELS:], ident_bf16[:])
-        gain = consts.tile([P, CHANNEL_TILES], F32)
-        nc.vector.tensor_copy(out=gain[:], in_=gain_ps[:, 0:CHANNEL_TILES])
+
+        def spread_bias():
+            bias_ps = psum_t.tile([P, CHANNELS], F32, name="zT_ps")
+            nc.tensor.matmul(bias_ps[:], lhsT=ones[:], rhs=rows[:], start=True, stop=True)
+            nc.vector.tensor_copy(out=bias[:], in_=bias_ps[:])
 
         codes = [per_chunk.tile([P, PASSES, CHUNK], U32, name="codes", align_bytes=64) for c in range(CHUNKS)]
         planes = [per_chunk.tile([P, PASSES, CHUNK], U8, name="planes", align_bytes=64) for c in range(CHUNKS)]
@@ -130,10 +125,9 @@ def tile_linearattention_pb_kernel(tc, h_attn, xn, Wout_words, Wout_scales, bout
             grouped[c, g] = staging.tile([P, CHUNK, PACK], BF16, name="grouped", align_bytes=64)
             to_words = grouped[c, g][:].rearrange("p (n i) t -> p n t i", i=RUN)
             from_rows = raw[c][:, g, :, :].rearrange("p t (n i) -> p n t i", i=RUN)
-            split = VECTOR_SHARE // RUN
+            split = VECTOR_SHARES[c] // RUN
             nc.vector.tensor_copy(out=to_words[:, :split], in_=from_rows[:, :split])
-            with tc.high_priority(offset=10000):
-                nc.scalar.copy(out=to_words[:, split:], in_=from_rows[:, split:])
+            nc.scalar.copy(out=to_words[:, split:], in_=from_rows[:, split:])
 
         def quantise(c, g):
             nc.vector.quantize_mx(
@@ -142,47 +136,39 @@ def tile_linearattention_pb_kernel(tc, h_attn, xn, Wout_words, Wout_scales, bout
                 in_=grouped[c, g][:].rearrange("p w t -> p (w t)"),
             )
 
-        def prepare(c):
-            regroup(c, 0)
-            for g in range(1, PASSES):
-                regroup(c, g)
-                quantise(c, g - 1)
-            quantise(c, PASSES - 1)
-
         y_ps, y_sb, z_sb, zT_ps = {}, {}, {}, {}
-        sums, squares, std, rstd, shift = {}, {}, {}, {}, {}
+        sums, squares, rstd, minus_mean = {}, {}, {}, {}
 
-        def project(c):
+        def open_chunk(c):
             y_ps[c] = [psum_y.tile([P, CHANNELS], F32, name="y_ps") for i in range(POSITION_TILES)]
-            for i in range(POSITION_TILES):
-                tile_cols = slice(i * P, (i + 1) * P)
-                for g in range(PASSES):
-                    nc.tensor.matmul_mx(
-                        out=y_ps[c][i][:],
-                        lhsT=codes[c][:, g, tile_cols].bitcast(FP8X4),
-                        lhsT_scale=planes[c][:, g, tile_cols],
-                        rhs=w_words[:, g, :].bitcast(FP4X4),
-                        rhs_scale=w_scales[:, g, :],
-                        start=(g == 0),
-                        stop=(g == PASSES - 1),
-                    )
+            y_sb[c] = stats.tile([P, POSITION_TILES, CHANNELS], F32, name="y_sb")
+            sums[c] = stats.tile([P, POSITION_TILES], F32, name="sums")
 
-        def add_bias(c):
-            y_sb[c] = work.tile([P, POSITION_TILES, CHANNELS], F32, name="y_sb")
-            sums[c] = work.tile([P, POSITION_TILES], F32, name="sums")
-            for i in range(POSITION_TILES):
-                nc.vector.scalar_tensor_tensor(
-                    out=y_sb[c][:, i, :],
-                    in0=y_ps[c][i][:],
-                    scalar=1.0,
-                    in1=bias[:],
-                    op0=ALU.mult,
-                    op1=ALU.add,
-                    accum_out=sums[c][:, i : i + 1],
-                )
+        def project(c, g, i):
+            tile_cols = slice(i * P, (i + 1) * P)
+            nc.tensor.matmul_mx(
+                out=y_ps[c][i][:],
+                lhsT=codes[c][:, g, tile_cols].bitcast(FP8X4),
+                lhsT_scale=planes[c][:, g, tile_cols],
+                rhs=w_words[:, g, :].bitcast(FP4X4),
+                rhs_scale=w_scales[:, g, :],
+                start=(g == 0),
+                stop=(g == PASSES - 1),
+            )
+
+        def add_bias(c, i):
+            nc.vector.scalar_tensor_tensor(
+                out=y_sb[c][:, i, :],
+                in0=y_ps[c][i][:],
+                scalar=1.0,
+                in1=bias[:],
+                op0=ALU.mult,
+                op1=ALU.add,
+                accum_out=sums[c][:, i : i + 1],
+            )
 
         def sum_squares(c):
-            squares[c] = work.tile([P, POSITION_TILES], F32, name="squares")
+            squares[c] = stats.tile([P, POSITION_TILES], F32, name="squares")
             for i in range(POSITION_TILES):
                 unread = scratch.tile([P, CHANNELS], BF16, name="unread")
                 nc.scalar.activation(
@@ -195,7 +181,7 @@ def tile_linearattention_pb_kernel(tc, h_attn, xn, Wout_words, Wout_scales, bout
                 )
 
         def standard_deviation(c):
-            rstd[c] = work.tile([P, POSITION_TILES], F32, name="rstd")
+            rstd[c] = stats.tile([P, POSITION_TILES], F32, name="rstd")
             nc.scalar.activation(
                 out=rstd[c][:],
                 in_=squares[c][:],
@@ -204,34 +190,21 @@ def tile_linearattention_pb_kernel(tc, h_attn, xn, Wout_words, Wout_scales, bout
                 scale=1.0 / CHANNELS**3,
             )
 
-        def scale_and_shift(c):
-            std[c] = work.tile([P, POSITION_TILES], F32, name="std")
-            nc.gpsimd.tensor_scalar(
-                out=std[c][:], in0=sums[c][:], scalar1=-1.0 / CHANNELS, scalar2=0.0, op0=ALU.mult, op1=ALU.add
-            )
-            shift[c] = work.tile([P, POSITION_TILES], F32, name="shift")
-            nc.gpsimd.tensor_tensor(out=shift[c][:], in0=std[c][:], in1=rstd[c][:], op=ALU.mult)
-
         def normalise(c):
+            minus_mean[c] = stats.tile([P, POSITION_TILES], F32, name="minus_mean")
+            nc.gpsimd.tensor_scalar(
+                out=minus_mean[c][:], in0=sums[c][:], scalar1=-1.0 / CHANNELS, scalar2=0.0, op0=ALU.mult, op1=ALU.add
+            )
             z_sb[c] = work.tile([P, POSITION_TILES, CHANNELS], F32, name="z_sb")
             for i in range(POSITION_TILES):
-                if i < POSITION_TILES - 1:
-                    nc.gpsimd.tensor_scalar(
-                        out=z_sb[c][:, i, :],
-                        in0=y_sb[c][:, i, :],
-                        scalar1=rstd[c][:, i : i + 1],
-                        scalar2=shift[c][:, i : i + 1],
-                        op0=ALU.mult,
-                        op1=ALU.add,
-                    )
-                else:
-                    nc.scalar.activation(
-                        out=z_sb[c][:, i, :],
-                        in_=y_sb[c][:, i, :],
-                        func=ACT.Identity,
-                        bias=shift[c][:, i : i + 1],
-                        scale=rstd[c][:, i : i + 1],
-                    )
+                nc.gpsimd.tensor_scalar(
+                    out=z_sb[c][:, i, :],
+                    in0=y_sb[c][:, i, :],
+                    scalar1=minus_mean[c][:, i : i + 1],
+                    scalar2=rstd[c][:, i : i + 1],
+                    op0=ALU.add,
+                    op1=ALU.mult,
+                )
 
         def transpose(c):
             zT_ps[c] = [psum_t.tile([P, CHUNK], F32, name="zT_ps") for ct in range(CHANNEL_TILES)]
@@ -257,23 +230,56 @@ def tile_linearattention_pb_kernel(tc, h_attn, xn, Wout_words, Wout_scales, bout
                 )
                 nc.sync.dma_start(out=out_dram[b, ct * P : (ct + 1) * P, cols], in_=result[:, ct, :])
 
-        prepare(0)
-        project(0)
-        prepare(1)
-        for step in range(CHUNKS + 2):
-            if 1 <= step <= CHUNKS:
-                standard_deviation(step - 1)
-            if step >= 2:
-                transpose(step - 2)
-            if step < CHUNKS:
-                add_bias(step)
-                sum_squares(step)
-            if step + 1 < CHUNKS:
-                project(step + 1)
-            if step + 2 < CHUNKS:
-                prepare(step + 2)
-            if 1 <= step <= CHUNKS:
-                scale_and_shift(step - 1)
-                normalise(step - 1)
-            if step >= 2:
-                finish(step - 2)
+        def normalised(c):
+            sum_squares(c)
+            standard_deviation(c)
+            normalise(c)
+
+        with tc.manual_schedule():
+            open_chunk(0)
+            regroup(0, 0)
+            regroup(0, 1)
+            quantise(0, 0)
+            regroup(0, 2)
+            quantise(0, 1)
+            quantise(0, 2)
+            spread_bias()
+            for g in range(PASSES):
+                for i in range(POSITION_TILES):
+                    project(0, g, i)
+
+            for c in range(1, CHUNKS):
+                regroup(c, 0)
+                regroup(c, 1)
+                if c == 1:
+                    add_bias(0, 0)
+                quantise(c, 0)
+                regroup(c, 2)
+                for g in range(1, PASSES):
+                    if c == 1:
+                        add_bias(0, g)
+                    quantise(c, g)
+                for i in range(POSITION_TILES) if c > 1 else [POSITION_TILES - 1]:
+                    add_bias(c - 1, i)
+                open_chunk(c)
+                if c < CHUNKS - 1:
+                    for g in range(PASSES):
+                        for i in range(POSITION_TILES):
+                            project(c, g, i)
+                else:
+                    for i in range(POSITION_TILES):
+                        for g in range(PASSES):
+                            project(c, g, i)
+
+            last = CHUNKS - 1
+            normalised(0)
+            transpose(0)
+            add_bias(last, 0)
+            add_bias(last, 1)
+            finish(0)
+            add_bias(last, 2)
+            add_bias(last, 3)
+            for c in range(1, CHUNKS):
+                normalised(c)
+                transpose(c)
+                finish(c)

@@ -27,7 +27,8 @@ CHUNK = 512
 POSITION_TILES = CHUNK // P
 CHUNKS_PER_IMAGE = POSITIONS // CHUNK
 CHUNKS = IMAGES * CHUNKS_PER_IMAGE
-VECTOR_SHARES = (272, 224, 192, 160)
+FIRST_SHARE = CHUNK // 2
+SHARE_STEP = 16
 RUN = 4
 EPS = 1e-5
 
@@ -110,10 +111,10 @@ def tile_linearattention_pb_kernel(tc, h_attn, xn, Wout_words, Wout_scales, bout
         load_residual(0)
         load_residual(1)
 
-        bias = consts.tile([P, CHANNELS], F32)
+        bias = consts.tile([P, CHANNELS], BF16)
 
         def spread_bias():
-            bias_ps = psum_t.tile([P, CHANNELS], F32, name="zT_ps")
+            bias_ps = psum_t.tile([P, CHANNELS], BF16, name="zT_ps")
             nc.tensor.matmul(bias_ps[:], lhsT=ones[:], rhs=rows[:], start=True, stop=True)
             nc.vector.tensor_copy(out=bias[:], in_=bias_ps[:])
 
@@ -125,7 +126,7 @@ def tile_linearattention_pb_kernel(tc, h_attn, xn, Wout_words, Wout_scales, bout
             grouped[c, g] = staging.tile([P, CHUNK, PACK], BF16, name="grouped", align_bytes=64)
             to_words = grouped[c, g][:].rearrange("p (n i) t -> p n t i", i=RUN)
             from_rows = raw[c][:, g, :, :].rearrange("p t (n i) -> p n t i", i=RUN)
-            split = VECTOR_SHARES[c] // RUN
+            split = (FIRST_SHARE - c * SHARE_STEP) // RUN
             nc.vector.tensor_copy(out=to_words[:, :split], in_=from_rows[:, :split])
             nc.scalar.copy(out=to_words[:, split:], in_=from_rows[:, split:])
 
@@ -137,7 +138,7 @@ def tile_linearattention_pb_kernel(tc, h_attn, xn, Wout_words, Wout_scales, bout
             )
 
         y_ps, y_sb, z_sb, zT_ps = {}, {}, {}, {}
-        sums, squares, rstd, minus_mean = {}, {}, {}, {}
+        sums, squares, rstd, minus_mean, shift = {}, {}, {}, {}, {}
 
         def open_chunk(c):
             y_ps[c] = [psum_y.tile([P, CHANNELS], F32, name="y_ps") for i in range(POSITION_TILES)]
@@ -195,16 +196,28 @@ def tile_linearattention_pb_kernel(tc, h_attn, xn, Wout_words, Wout_scales, bout
             nc.gpsimd.tensor_scalar(
                 out=minus_mean[c][:], in0=sums[c][:], scalar1=-1.0 / CHANNELS, scalar2=0.0, op0=ALU.mult, op1=ALU.add
             )
+            if c == CHUNKS - 1:
+                shift[c] = stats.tile([P, POSITION_TILES], F32, name="shift")
+                nc.gpsimd.tensor_tensor(out=shift[c][:], in0=minus_mean[c][:], in1=rstd[c][:], op=ALU.mult)
             z_sb[c] = work.tile([P, POSITION_TILES, CHANNELS], F32, name="z_sb")
             for i in range(POSITION_TILES):
-                nc.gpsimd.tensor_scalar(
-                    out=z_sb[c][:, i, :],
-                    in0=y_sb[c][:, i, :],
-                    scalar1=minus_mean[c][:, i : i + 1],
-                    scalar2=rstd[c][:, i : i + 1],
-                    op0=ALU.add,
-                    op1=ALU.mult,
-                )
+                if c == CHUNKS - 1 and i != 1:
+                    nc.scalar.activation(
+                        out=z_sb[c][:, i, :],
+                        in_=y_sb[c][:, i, :],
+                        func=ACT.Identity,
+                        bias=shift[c][:, i : i + 1],
+                        scale=rstd[c][:, i : i + 1],
+                    )
+                else:
+                    nc.gpsimd.tensor_scalar(
+                        out=z_sb[c][:, i, :],
+                        in0=y_sb[c][:, i, :],
+                        scalar1=minus_mean[c][:, i : i + 1],
+                        scalar2=rstd[c][:, i : i + 1],
+                        op0=ALU.add,
+                        op1=ALU.mult,
+                    )
 
         def transpose(c):
             zT_ps[c] = [psum_t.tile([P, CHUNK], F32, name="zT_ps") for ct in range(CHANNEL_TILES)]
@@ -230,56 +243,67 @@ def tile_linearattention_pb_kernel(tc, h_attn, xn, Wout_words, Wout_scales, bout
                 )
                 nc.sync.dma_start(out=out_dram[b, ct * P : (ct + 1) * P, cols], in_=result[:, ct, :])
 
-        def normalised(c):
+        def empty(c, tiles):
+            for i in tiles:
+                add_bias(c, i)
+
+        def project_chunk(c):
+            open_chunk(c)
+            for i in range(POSITION_TILES):
+                for g in range(PASSES):
+                    project(c, g, i)
+
+        def normalise_chunk(c):
             sum_squares(c)
             standard_deviation(c)
             normalise(c)
 
         with tc.manual_schedule():
-            open_chunk(0)
             regroup(0, 0)
             regroup(0, 1)
             quantise(0, 0)
             regroup(0, 2)
             quantise(0, 1)
-            quantise(0, 2)
             spread_bias()
-            for g in range(PASSES):
-                for i in range(POSITION_TILES):
-                    project(0, g, i)
+            quantise(0, 2)
+            project_chunk(0)
 
-            for c in range(1, CHUNKS):
-                regroup(c, 0)
-                regroup(c, 1)
-                if c == 1:
-                    add_bias(0, 0)
-                quantise(c, 0)
-                regroup(c, 2)
-                for g in range(1, PASSES):
-                    if c == 1:
-                        add_bias(0, g)
-                    quantise(c, g)
-                for i in range(POSITION_TILES) if c > 1 else [POSITION_TILES - 1]:
-                    add_bias(c - 1, i)
-                open_chunk(c)
-                if c < CHUNKS - 1:
-                    for g in range(PASSES):
-                        for i in range(POSITION_TILES):
-                            project(c, g, i)
-                else:
-                    for i in range(POSITION_TILES):
-                        for g in range(PASSES):
-                            project(c, g, i)
+            regroup(1, 0)
+            regroup(1, 1)
+            quantise(1, 0)
+            regroup(1, 2)
+            empty(0, (0, 1))
+            quantise(1, 1)
+            empty(0, (2,))
+            quantise(1, 2)
+            empty(0, (3,))
+            project_chunk(1)
 
-            last = CHUNKS - 1
-            normalised(0)
+            regroup(2, 0)
+            regroup(2, 1)
+            quantise(2, 0)
+            regroup(2, 2)
+            quantise(2, 1)
+            quantise(2, 2)
+            empty(1, (0, 1, 2, 3))
+            project_chunk(2)
+            normalise_chunk(0)
             transpose(0)
-            add_bias(last, 0)
-            add_bias(last, 1)
+
+            regroup(3, 0)
+            regroup(3, 1)
+            quantise(3, 0)
+            regroup(3, 2)
+            quantise(3, 1)
+            empty(2, (0, 1))
+            quantise(3, 2)
+            empty(2, (2, 3))
+            project_chunk(3)
             finish(0)
-            add_bias(last, 2)
-            add_bias(last, 3)
+            normalise_chunk(1)
+            empty(3, (0, 1, 2, 3))
             for c in range(1, CHUNKS):
-                normalised(c)
+                if c > 1:
+                    normalise_chunk(c)
                 transpose(c)
                 finish(c)

@@ -168,9 +168,10 @@ def tile_linearattention_pb_kernel(tc, h_attn, xn, Wout_words, Wout_scales, bout
                 accum_out=sums[c][:, i : i + 1],
             )
 
-        def sum_squares(c):
-            squares[c] = stats.tile([P, POSITION_TILES], F32, name="squares")
-            for i in range(POSITION_TILES):
+        def sum_squares(c, tiles):
+            if c not in squares:
+                squares[c] = stats.tile([P, POSITION_TILES], F32, name="squares")
+            for i in tiles:
                 unread = scratch.tile([P, CHANNELS], BF16, name="unread")
                 nc.scalar.activation(
                     out=unread[:],
@@ -191,25 +192,19 @@ def tile_linearattention_pb_kernel(tc, h_attn, xn, Wout_words, Wout_scales, bout
                 scale=1.0 / CHANNELS**3,
             )
 
-        def normalise(c):
+        def scalar_tiles(c):
+            return (0, 2, 3) if c == CHUNKS - 1 else (3,)
+
+        def normalise_on_gpsimd(c):
             minus_mean[c] = stats.tile([P, POSITION_TILES], F32, name="minus_mean")
             nc.gpsimd.tensor_scalar(
                 out=minus_mean[c][:], in0=sums[c][:], scalar1=-1.0 / CHANNELS, scalar2=0.0, op0=ALU.mult, op1=ALU.add
             )
-            if c == CHUNKS - 1:
-                shift[c] = stats.tile([P, POSITION_TILES], F32, name="shift")
-                nc.gpsimd.tensor_tensor(out=shift[c][:], in0=minus_mean[c][:], in1=rstd[c][:], op=ALU.mult)
+            shift[c] = stats.tile([P, POSITION_TILES], F32, name="shift")
+            nc.gpsimd.tensor_tensor(out=shift[c][:], in0=minus_mean[c][:], in1=rstd[c][:], op=ALU.mult)
             z_sb[c] = work.tile([P, POSITION_TILES, CHANNELS], F32, name="z_sb")
             for i in range(POSITION_TILES):
-                if c == CHUNKS - 1 and i != 1:
-                    nc.scalar.activation(
-                        out=z_sb[c][:, i, :],
-                        in_=y_sb[c][:, i, :],
-                        func=ACT.Identity,
-                        bias=shift[c][:, i : i + 1],
-                        scale=rstd[c][:, i : i + 1],
-                    )
-                else:
+                if i not in scalar_tiles(c):
                     nc.gpsimd.tensor_scalar(
                         out=z_sb[c][:, i, :],
                         in0=y_sb[c][:, i, :],
@@ -218,6 +213,16 @@ def tile_linearattention_pb_kernel(tc, h_attn, xn, Wout_words, Wout_scales, bout
                         op0=ALU.add,
                         op1=ALU.mult,
                     )
+
+        def normalise_on_scalar(c):
+            for i in scalar_tiles(c):
+                nc.scalar.activation(
+                    out=z_sb[c][:, i, :],
+                    in_=y_sb[c][:, i, :],
+                    func=ACT.Identity,
+                    bias=shift[c][:, i : i + 1],
+                    scale=rstd[c][:, i : i + 1],
+                )
 
         def transpose(c):
             zT_ps[c] = [psum_t.tile([P, CHUNK], F32, name="zT_ps") for ct in range(CHANNEL_TILES)]
@@ -253,11 +258,6 @@ def tile_linearattention_pb_kernel(tc, h_attn, xn, Wout_words, Wout_scales, bout
                 for g in range(PASSES):
                     project(c, g, i)
 
-        def normalise_chunk(c):
-            sum_squares(c)
-            standard_deviation(c)
-            normalise(c)
-
         with tc.manual_schedule():
             regroup(0, 0)
             regroup(0, 1)
@@ -287,10 +287,14 @@ def tile_linearattention_pb_kernel(tc, h_attn, xn, Wout_words, Wout_scales, bout
             quantise(2, 2)
             empty(1, (0, 1, 2, 3))
             project_chunk(2)
-            normalise_chunk(0)
+            all_tiles = range(POSITION_TILES)
+            sum_squares(0, all_tiles)
+            standard_deviation(0)
+            normalise_on_gpsimd(0)
+            regroup(3, 0)
+            normalise_on_scalar(0)
             transpose(0)
 
-            regroup(3, 0)
             regroup(3, 1)
             quantise(3, 0)
             regroup(3, 2)
@@ -300,10 +304,15 @@ def tile_linearattention_pb_kernel(tc, h_attn, xn, Wout_words, Wout_scales, bout
             empty(2, (2, 3))
             project_chunk(3)
             finish(0)
-            normalise_chunk(1)
-            empty(3, (0, 1, 2, 3))
+            sum_squares(1, all_tiles)
+            empty(3, all_tiles)
             for c in range(1, CHUNKS):
-                if c > 1:
-                    normalise_chunk(c)
+                standard_deviation(c)
+                normalise_on_gpsimd(c)
+                if c + 1 < CHUNKS:
+                    sum_squares(c + 1, all_tiles[:1])
+                normalise_on_scalar(c)
                 transpose(c)
                 finish(c)
+                if c + 1 < CHUNKS:
+                    sum_squares(c + 1, all_tiles[1:])

@@ -52,6 +52,20 @@ def tile_linearattention_pb_kernel(tc, h_attn, xn, Wout_words, Wout_scales, bout
         psum_y = ctx.enter_context(tc.psum_pool(name="psum_y", bufs=POSITION_TILES))
         psum_t = ctx.enter_context(tc.psum_pool(name="psum_t", bufs=CHANNEL_TILES))
 
+        w_scales = consts.tile([P, PASSES, CHANNELS], U8, align_bytes=64)
+        nc.vector.memset(w_scales[:].bitcast(I32), 0)
+        for quadrant in range(4):
+            nc.sync.dma_start(
+                out=w_scales[32 * quadrant : 32 * quadrant + 4, :, :].bitcast(I32),
+                in_=Wout_scales[:, 4 * quadrant : 4 * quadrant + 4, :]
+                .bitcast(I32)
+                .rearrange("g r n -> r g n"),
+            )
+
+        rows = consts.tile([P, CHANNELS], BF16)
+        nc.vector.memset(rows[:], 0.0)
+        nc.sync.dma_start(out=rows[0:1, :], in_=bout.rearrange("(o c) -> o c", o=1))
+
         ident_f32 = consts.tile([P, P], F32)
         make_identity(nc, ident_f32[:])
         ones = consts.tile([P, P], BF16)
@@ -60,9 +74,6 @@ def tile_linearattention_pb_kernel(tc, h_attn, xn, Wout_words, Wout_scales, bout
         nc.vector.memset(eps[:], EPS)
         warm = consts.tile([P, 1], F32)
         nc.scalar.activation(out=warm[:], in_=eps[:], func=ACT.Abs_reciprocal_sqrt)
-
-        rows = consts.tile([P, CHANNELS], BF16)
-        nc.vector.memset(rows[:], 0.0)
 
         raw = []
         xn_sb = []
@@ -87,22 +98,11 @@ def tile_linearattention_pb_kernel(tc, h_attn, xn, Wout_words, Wout_scales, bout
             xn_sb.append(xn_b)
 
         load_chunk(0)
-        nc.sync.dma_start(out=rows[0:1, :], in_=bout.rearrange("(o c) -> o c", o=1))
 
         w_words = consts.tile([P, PASSES, 2 * CHANNELS], U8, align_bytes=64)
         nc.sync.dma_start(
             out=w_words[:].bitcast(I32), in_=Wout_words.bitcast(I32).rearrange("g p n -> p g n")
         )
-        w_scales = consts.tile([P, PASSES, CHANNELS], U8, align_bytes=64)
-        nc.vector.memset(w_scales[:].bitcast(I32), 0)
-        for quadrant in range(4):
-            nc.sync.dma_start(
-                out=w_scales[32 * quadrant : 32 * quadrant + 4, :, :].bitcast(I32),
-                in_=Wout_scales[:, 4 * quadrant : 4 * quadrant + 4, :]
-                .bitcast(I32)
-                .rearrange("g r n -> r g n"),
-            )
-
         load_chunk(1)
         load_chunk(2)
         load_chunk(3)
@@ -264,19 +264,20 @@ def tile_linearattention_pb_kernel(tc, h_attn, xn, Wout_words, Wout_scales, bout
             quantise(0, 0)
             regroup(0, 2)
             quantise(0, 1)
-            spread_bias()
             quantise(0, 2)
+            regroup(1, 0)
+            spread_bias()
             project_chunk(0)
 
-            regroup(1, 0)
+            empty(0, (0,))
             regroup(1, 1)
             quantise(1, 0)
+            empty(0, (1,))
             regroup(1, 2)
-            empty(0, (0, 1))
-            quantise(1, 1)
             empty(0, (2,))
-            quantise(1, 2)
+            quantise(1, 1)
             empty(0, (3,))
+            quantise(1, 2)
             project_chunk(1)
 
             regroup(2, 0)

from contextlib import ExitStack

import concourse.mybir as mybir
from concourse.masks import make_identity

F32 = mybir.dt.float32
BF16 = mybir.dt.bfloat16
I32 = mybir.dt.int32
U32 = mybir.dt.uint32
U8 = mybir.dt.uint8
FP8X4 = mybir.dt.float8_e4m3fn_x4
FP4X4 = mybir.dt.float4_e2m1fn_x4
ALU = mybir.AluOpType
ACT = mybir.ActivationFunctionType

P = 128
PACK = 4
K_PASS = P * PACK

IMAGES = 2
K = 1536
PASSES = K // K_PASS
CHANNELS = 512
CHANNEL_TILES = CHANNELS // P
POSITIONS = 1024
CHUNK = 512
POSITION_TILES = CHUNK // P
CHUNKS_PER_IMAGE = POSITIONS // CHUNK
CHUNKS = IMAGES * CHUNKS_PER_IMAGE
FIRST_SHARE = CHUNK // 2
SHARE_STEP = 16
RUN = 4
EPS = 1e-5

FLOPS = 2 * IMAGES * POSITIONS * CHANNELS * K


def tile_linearattention_pb_kernel(tc, h_attn, xn, Wout_words, Wout_scales, bout, outnorm_g, out):
    nc = tc.nc
    h_dram = h_attn.rearrange("b k h w -> b k (h w)")
    xn_dram = xn.rearrange("b c h w -> b c (h w)")
    out_dram = out.rearrange("b c h w -> b c (h w)")

    with ExitStack() as ctx:
        consts = ctx.enter_context(tc.tile_pool(name="consts", bufs=1))
        per_image = ctx.enter_context(tc.tile_pool(name="per_image", bufs=IMAGES))
        per_chunk = ctx.enter_context(tc.tile_pool(name="per_chunk", bufs=CHUNKS))
        work = ctx.enter_context(tc.tile_pool(name="work", bufs=3))
        staging = ctx.enter_context(tc.tile_pool(name="staging", bufs=2 * PASSES))
        stats = ctx.enter_context(tc.tile_pool(name="stats", bufs=CHUNKS))
        scratch = ctx.enter_context(tc.tile_pool(name="scratch", bufs=POSITION_TILES))
        psum_y = ctx.enter_context(tc.psum_pool(name="psum_y", bufs=POSITION_TILES))
        psum_t = ctx.enter_context(tc.psum_pool(name="psum_t", bufs=CHANNEL_TILES))

        w_scales = consts.tile([P, PASSES, CHANNELS], U8, align_bytes=64)
        nc.vector.memset(w_scales[:].bitcast(I32), 0)
        for quadrant in range(4):
            nc.sync.dma_start(
                out=w_scales[32 * quadrant : 32 * quadrant + 4, :, :].bitcast(I32),
                in_=Wout_scales[:, 4 * quadrant : 4 * quadrant + 4, :]
                .bitcast(I32)
                .rearrange("g r n -> r g n"),
            )

        rows = consts.tile([P, CHANNELS], BF16)
        nc.vector.memset(rows[:], 0.0)
        nc.sync.dma_start(out=rows[0:1, :], in_=bout.rearrange("(o c) -> o c", o=1))

        ident_f32 = consts.tile([P, P], F32)
        make_identity(nc, ident_f32[:])
        ones = consts.tile([P, P], BF16)
        nc.vector.memset(ones[:], 1.0)
        eps = consts.tile([P, 1], F32)
        nc.vector.memset(eps[:], EPS)
        warm = consts.tile([P, 1], F32)
        nc.scalar.activation(out=warm[:], in_=eps[:], func=ACT.Abs_reciprocal_sqrt)

        raw = []
        xn_sb = []

        def image_and_columns(c):
            first = (c % CHUNKS_PER_IMAGE) * CHUNK
            return c // CHUNKS_PER_IMAGE, slice(first, first + CHUNK)

        def load_chunk(c):
            b, cols = image_and_columns(c)
            raw_c = per_chunk.tile([P, PASSES, PACK, CHUNK], BF16, name="raw_c")
            for g in range(PASSES):
                k_rows = slice(g * K_PASS, (g + 1) * K_PASS)
                nc.sync.dma_start(
                    out=raw_c[:, g, :, :], in_=h_dram[b, k_rows, cols].rearrange("(p t) w -> p t w", t=PACK)
                )
            raw.append(raw_c)

        def load_residual(b):
            xn_b = per_image.tile([P, CHANNEL_TILES, POSITIONS], BF16, name="xn_b")
            nc.sync.dma_start(out=xn_b[:], in_=xn_dram[b].rearrange("(ct p) w -> p ct w", p=P))
            xn_sb.append(xn_b)

        load_chunk(0)

        w_words = consts.tile([P, PASSES, 2 * CHANNELS], U8, align_bytes=64)
        nc.sync.dma_start(
            out=w_words[:].bitcast(I32), in_=Wout_words.bitcast(I32).rearrange("g p n -> p g n")
        )
        load_chunk(1)
        load_chunk(2)
        load_chunk(3)
        gain = consts.tile([P, CHANNEL_TILES], BF16)
        nc.sync.dma_start(out=gain[:], in_=outnorm_g.rearrange("o (ct p) h w -> p (o ct h w)", p=P))
        load_residual(0)
        load_residual(1)

        bias = consts.tile([P, CHANNELS], BF16)

        def spread_bias():
            bias_ps = psum_t.tile([P, CHANNELS], BF16, name="zT_ps")
            nc.tensor.matmul(bias_ps[:], lhsT=ones[:], rhs=rows[:], start=True, stop=True)
            nc.vector.tensor_copy(out=bias[:], in_=bias_ps[:])

        codes = [per_chunk.tile([P, PASSES, CHUNK], U32, name="codes", align_bytes=64) for c in range(CHUNKS)]
        planes = [per_chunk.tile([P, PASSES, CHUNK], U8, name="planes", align_bytes=64) for c in range(CHUNKS)]
        grouped = {}

        def regroup(c, g):
            grouped[c, g] = staging.tile([P, CHUNK, PACK], BF16, name="grouped", align_bytes=64)
            to_words = grouped[c, g][:].rearrange("p (n i) t -> p n t i", i=RUN)
            from_rows = raw[c][:, g, :, :].rearrange("p t (n i) -> p n t i", i=RUN)
            split = (FIRST_SHARE - c * SHARE_STEP) // RUN
            nc.vector.tensor_copy(out=to_words[:, :split], in_=from_rows[:, :split])
            nc.scalar.copy(out=to_words[:, split:], in_=from_rows[:, split:])

        def quantise(c, g):
            nc.vector.quantize_mx(
                out=codes[c][:, g, :].bitcast(FP8X4),
                scales=planes[c][:, g, :],
                in_=grouped[c, g][:].rearrange("p w t -> p (w t)"),
            )

        y_ps, y_sb, z_sb, zT_ps = {}, {}, {}, {}
        sums, squares, rstd, minus_mean, shift = {}, {}, {}, {}, {}

        def open_chunk(c):
            y_ps[c] = [psum_y.tile([P, CHANNELS], F32, name="y_ps") for i in range(POSITION_TILES)]
            y_sb[c] = stats.tile([P, POSITION_TILES, CHANNELS], F32, name="y_sb")
            sums[c] = stats.tile([P, POSITION_TILES], F32, name="sums")

        def project(c, g, i):
            tile_cols = slice(i * P, (i + 1) * P)
            nc.tensor.matmul_mx(
                out=y_ps[c][i][:],
                lhsT=codes[c][:, g, tile_cols].bitcast(FP8X4),
                lhsT_scale=planes[c][:, g, tile_cols],
                rhs=w_words[:, g, :].bitcast(FP4X4),
                rhs_scale=w_scales[:, g, :],
                start=(g == 0),
                stop=(g == PASSES - 1),
            )

        def add_bias(c, i):
            nc.vector.scalar_tensor_tensor(
                out=y_sb[c][:, i, :],
                in0=y_ps[c][i][:],
                scalar=1.0,
                in1=bias[:],
                op0=ALU.mult,
                op1=ALU.add,
                accum_out=sums[c][:, i : i + 1],
            )

        def sum_squares(c, tiles):
            if c not in squares:
                squares[c] = stats.tile([P, POSITION_TILES], F32, name="squares")
            for i in tiles:
                unread = scratch.tile([P, CHANNELS], BF16, name="unread")
                nc.scalar.activation(
                    out=unread[:],
                    in_=y_sb[c][:, i, :],
                    func=ACT.Square,
                    bias=sums[c][:, i : i + 1],
                    scale=-1.0 * CHANNELS,
                    accum_out=squares[c][:, i : i + 1],
                )

        def standard_deviation(c):
            rstd[c] = stats.tile([P, POSITION_TILES], F32, name="rstd")
            nc.scalar.activation(
                out=rstd[c][:],
                in_=squares[c][:],
                func=ACT.Abs_reciprocal_sqrt,
                bias=eps[:],
                scale=1.0 / CHANNELS**3,
            )

        def scalar_tiles(c):
            return (0, 2, 3) if c == CHUNKS - 1 else (3,)

        def normalise_on_gpsimd(c):
            minus_mean[c] = stats.tile([P, POSITION_TILES], F32, name="minus_mean")
            nc.gpsimd.tensor_scalar(
                out=minus_mean[c][:], in0=sums[c][:], scalar1=-1.0 / CHANNELS, scalar2=0.0, op0=ALU.mult, op1=ALU.add
            )
            shift[c] = stats.tile([P, POSITION_TILES], F32, name="shift")
            nc.gpsimd.tensor_tensor(out=shift[c][:], in0=minus_mean[c][:], in1=rstd[c][:], op=ALU.mult)
            z_sb[c] = work.tile([P, POSITION_TILES, CHANNELS], F32, name="z_sb")
            for i in range(POSITION_TILES):
                if i not in scalar_tiles(c):
                    nc.gpsimd.tensor_scalar(
                        out=z_sb[c][:, i, :],
                        in0=y_sb[c][:, i, :],
                        scalar1=minus_mean[c][:, i : i + 1],
                        scalar2=rstd[c][:, i : i + 1],
                        op0=ALU.add,
                        op1=ALU.mult,
                    )

        def normalise_on_scalar(c):
            for i in scalar_tiles(c):
                nc.scalar.activation(
                    out=z_sb[c][:, i, :],
                    in_=y_sb[c][:, i, :],
                    func=ACT.Identity,
                    bias=shift[c][:, i : i + 1],
                    scale=rstd[c][:, i : i + 1],
                )

        def transpose(c):
            zT_ps[c] = [psum_t.tile([P, CHUNK], F32, name="zT_ps") for ct in range(CHANNEL_TILES)]
            for ct in range(CHANNEL_TILES):
                for i in range(POSITION_TILES):
                    nc.tensor.transpose(
                        zT_ps[c][ct][:, i * P : (i + 1) * P],
                        z_sb[c][:, i, ct * P : (ct + 1) * P],
                        ident_f32[:],
                    )

        def finish(c):
            b, cols = image_and_columns(c)
            result = work.tile([P, CHANNEL_TILES, CHUNK], F32, name="result")
            for ct in range(CHANNEL_TILES):
                nc.vector.scalar_tensor_tensor(
                    out=result[:, ct, :],
                    in0=zT_ps[c][ct][:],
                    scalar=gain[:, ct : ct + 1],
                    in1=xn_sb[b][:, ct, cols],
                    op0=ALU.mult,
                    op1=ALU.add,
                )
                nc.sync.dma_start(out=out_dram[b, ct * P : (ct + 1) * P, cols], in_=result[:, ct, :])

        def empty(c, tiles):
            for i in tiles:
                add_bias(c, i)

        def project_chunk(c):
            open_chunk(c)
            for i in range(POSITION_TILES):
                for g in range(PASSES):
                    project(c, g, i)

        with tc.manual_schedule():
            regroup(0, 0)
            regroup(0, 1)
            quantise(0, 0)
            regroup(0, 2)
            quantise(0, 1)
            quantise(0, 2)
            regroup(1, 0)
            spread_bias()
            project_chunk(0)

            empty(0, (0,))
            regroup(1, 1)
            quantise(1, 0)
            empty(0, (1,))
            regroup(1, 2)
            empty(0, (2,))
            quantise(1, 1)
            empty(0, (3,))
            quantise(1, 2)
            project_chunk(1)

            regroup(2, 0)
            regroup(2, 1)
            quantise(2, 0)
            regroup(2, 2)
            quantise(2, 1)
            quantise(2, 2)
            empty(1, (0, 1, 2, 3))
            project_chunk(2)
            all_tiles = range(POSITION_TILES)
            sum_squares(0, all_tiles)
            standard_deviation(0)
            normalise_on_gpsimd(0)
            regroup(3, 0)
            normalise_on_scalar(0)
            transpose(0)

            regroup(3, 1)
            quantise(3, 0)
            regroup(3, 2)
            quantise(3, 1)
            empty(2, (0, 1))
            quantise(3, 2)
            empty(2, (2, 3))
            project_chunk(3)
            finish(0)
            sum_squares(1, all_tiles)
            empty(3, all_tiles)
            for c in range(1, CHUNKS):
                standard_deviation(c)
                normalise_on_gpsimd(c)
                if c + 1 < CHUNKS:
                    sum_squares(c + 1, all_tiles[:1])
                normalise_on_scalar(c)
                transpose(c)
                finish(c)
                if c + 1 < CHUNKS:
                    sum_squares(c + 1, all_tiles[1:])
